import numpy as np
import ml_dtypes


def mxq(x, axis, fmt="e4m3"):
    dtype, down = {"e4m3": (ml_dtypes.float8_e4m3fn, 7), "e5m2": (ml_dtypes.float8_e5m2, 14)}[fmt]
    v = np.moveaxis(np.asarray(x, np.float32).astype(ml_dtypes.bfloat16).astype(np.float64), axis, -1)
    blocks = v.reshape(v.shape[:-1] + (-1, 32))
    amax = np.abs(blocks).max(-1, keepdims=True)
    byte = np.maximum(np.where(amax > 0, np.frexp(amax)[1] - 1 + 127, 0) - down, 1)
    scale = np.exp2(byte - 127.0)
    codes = (blocks / scale).astype(np.float32).astype(dtype).astype(np.float64)
    return np.moveaxis((codes * scale).reshape(v.shape), -1, axis)


WIDE = False


def mx_kscale(k):
    if not WIDE:
        return np.ones(k)
    levels = np.array([10, -10, 5, -5, 0])
    a = np.random.permutation(np.resize(levels, k // 512 * 4)).reshape(k // 512, 4)
    idx = np.arange(k)
    return np.exp2(a[idx // 512, idx % 128 // 32])


BF16 = ml_dtypes.bfloat16


def bf(x):
    return np.asarray(x, np.float32).astype(BF16)


def f64(x):
    return np.asarray(x).astype(np.float64)


E2M1 = np.array([0.0, 0.5, 1.0, 1.5, 2.0, 3.0, 4.0, 6.0, -0.0, -0.5, -1.0, -1.5, -2.0, -3.0, -4.0, -6.0])


def pack_weight(w, fmt):
    k, n = w.shape
    w = f64(bf(w)).reshape(k // 32, 32, n)
    amax = np.abs(w).max(1)
    if fmt == "e4m3":
        byte = np.frexp(amax)[1] - 1 + 127 - 7
    else:
        mant, ex = np.frexp(amax / 6.0)
        byte = np.where(mant > 0.5, ex, ex - 1) + 127
    byte = np.clip(np.where(amax > 0, byte, 1), 1, 254)
    scaled = (w * np.exp2(127.0 - byte)[:, None, :]).reshape(k, n).astype(np.float32)
    by_word = np.ascontiguousarray(scaled.reshape(k // 512, 128, 4, n).transpose(0, 1, 3, 2))
    if fmt == "e4m3":
        words = by_word.astype(ml_dtypes.float8_e4m3fn).view(np.uint8)
    else:
        c = by_word.astype(ml_dtypes.float4_e2m1fn).view(np.uint8) & 0xF
        words = c[..., 0::2] | (c[..., 1::2] << 4)
    return np.ascontiguousarray(words), np.ascontiguousarray(byte.astype(np.uint8).reshape(k // 512, 16, n))


def unpack_weight(words, scales, fmt):
    g, p, n, _ = words.shape
    if fmt == "e4m3":
        vals = np.ascontiguousarray(words).view(ml_dtypes.float8_e4m3fn).astype(np.float64)
    else:
        nib = np.empty((g, p, n, 4), np.uint8)
        nib[..., 0::2] = words & 0xF
        nib[..., 1::2] = words >> 4
        vals = E2M1[nib]
    vals = vals * np.repeat(np.exp2(scales.astype(np.float64) - 127.0), 8, axis=1)[..., None]
    return vals.transpose(0, 1, 3, 2).reshape(g * 512, n)

def pack4(w):
    words, scales = pack_weight(w, "e2m1")
    return words.reshape(words.shape[0], 128, -1), scales


def unpack4(words, scales):
    return unpack_weight(words.reshape(words.shape[0], 128, -1, 2), scales, "e2m1")


B, S, D, E, HD = 2, 128, 16384, 512, 64
ROPE_BASE = 10000.0


def rope_tables():
    inv_freq = 1.0 / ROPE_BASE ** (np.arange(0, E, 2) / E)
    ang = np.repeat(np.arange(S)[:, None] * inv_freq[None, :], 2, axis=-1)
    return np.cos(ang), np.sin(ang)


def rotate_half(v):
    h = v.shape[-1] // 2
    return np.concatenate([-v[..., h:], v[..., :h]], axis=-1)


def setup_inputs():
    s = mx_kscale(D)
    x = bf(np.random.standard_normal((B, S, D)) * s)
    Wq_words, Wq_scales = pack4(np.random.standard_normal((D, E)) * 0.5 / np.sqrt(D) / s[:, None])
    bq = bf(np.random.standard_normal(E) * 0.1)
    Wk_words, Wk_scales = pack4(np.random.standard_normal((D, E)) * 0.5 / np.sqrt(D) / s[:, None])
    bk = bf(np.random.standard_normal(E) * 0.1)
    return {"x": x,
            "Wq_words": Wq_words,
            "Wq_scales": Wq_scales,
            "bq": bq,
            "Wk_words": Wk_words,
            "Wk_scales": Wk_scales,
            "bk": bk}


def reference(x, Wq_words, Wq_scales, bq, Wk_words, Wk_scales, bk):
    xq = mxq(f64(x), 2, "e4m3")
    q = (xq @ unpack4(Wq_words, Wq_scales)) + f64(bq)
    k = (xq @ unpack4(Wk_words, Wk_scales)) + f64(bk)
    cos, sin = rope_tables()
    qr = q * cos + rotate_half(q) * sin
    kr = k * cos + rotate_half(k) * sin
    return qr, kr

@@ -1,0 +1,267 @@
+import math
+from contextlib import ExitStack
+
+import concourse.mybir as mybir
+from concourse.masks import make_identity
+
+F32 = mybir.dt.float32
+BF16 = mybir.dt.bfloat16
+I32 = mybir.dt.int32
+U32 = mybir.dt.uint32
+U8 = mybir.dt.uint8
+FP8X4 = mybir.dt.float8_e4m3fn_x4
+FP4X4 = mybir.dt.float4_e2m1fn_x4
+ALU = mybir.AluOpType
+ACT = mybir.ActivationFunctionType
+
+P = 128
+PACK = 4
+K_GROUP = P * PACK
+SEQUENCES = 2
+K = 16384
+GROUPS = K // K_GROUP
+FEATURES = 512
+HALF = FEATURES // 2
+PAIRS = FEATURES // 2
+PAIR_BITS = 8
+assert 2**PAIR_BITS == PAIRS
+ROPE_BASE = 10000.0
+
+ROUND = 4
+ROUNDS = GROUPS // ROUND
+ROUND_K = ROUND * K_GROUP
+SCALE_ROUNDS = 2
+LAST_ROUNDS = 2
+
+TWO_PI = 2.0 * math.pi
+TWO_PI_HIGH = 6.28125
+TWO_PI_LOW = TWO_PI - TWO_PI_HIGH
+ROUND_TO_INTEGER = 12582912.0
+
+FLOPS = 2 * SEQUENCES * P * K * 2 * FEATURES
+
+
+def tile_ropemultiheadattention_pa_k_kernel(
+    tc, x, Wq_words, Wq_scales, bq, Wk_words, Wk_scales, bk, out_0, out_1
+):
+    nc = tc.nc
+    dram_words = {"q": Wq_words.bitcast(I32), "k": Wk_words.bitcast(I32)}
+    dram_scales = {"q": Wq_scales.bitcast(I32), "k": Wk_scales.bitcast(I32)}
+    dram_bias = {"q": bq, "k": bk}
+    dram_out = {"q": out_0, "k": out_1}
+
+    with ExitStack() as ctx:
+        keep = ctx.enter_context(tc.tile_pool(name="keep", bufs=1))
+        raw_pool = ctx.enter_context(tc.tile_pool(name="raw", bufs=3))
+        sorted_pool = ctx.enter_context(tc.tile_pool(name="sorted", bufs=2))
+        grouped_pool = ctx.enter_context(tc.tile_pool(name="grouped", bufs=2))
+        rope_pool = ctx.enter_context(tc.tile_pool(name="rope", bufs=2))
+        acc_pool = ctx.enter_context(tc.psum_pool(name="acc", bufs=1))
+        bank_pool = ctx.enter_context(tc.psum_pool(name="bank", bufs=4))
+        ctx.enter_context(tc.manual_schedule())
+
+        w_words = {}
+        x_words = {}
+        x_planes = {}
+        for r in range(ROUNDS):
+            for w in ("q", "k"):
+                w_words[(w, r)] = keep.tile(
+                    [P, ROUND, 2 * FEATURES], U8, name="w_words_%s%d" % (w, r), align_bytes=64
+                )
+            x_words[r] = keep.tile([P, ROUND, SEQUENCES, P], U32, name="x_words_%d" % r, align_bytes=64)
+            x_planes[r] = keep.tile([P, ROUND, SEQUENCES, P], U8, name="x_planes_%d" % r, align_bytes=64)
+        w_planes = {}
+        for run in range(ROUNDS // SCALE_ROUNDS):
+            w_planes[run] = keep.tile(
+                [P, SCALE_ROUNDS * ROUND, FEATURES], U8, name="w_planes_%d" % run, align_bytes=64
+            )
+        acc = {}
+        for w in ("q", "k"):
+            for m in range(SEQUENCES):
+                acc[(w, m)] = acc_pool.tile([P, FEATURES], F32, name="acc_%s%d" % (w, m))
+
+        identity = keep.tile([P, P], F32, name="identity")
+        ones = keep.tile([P, P], BF16, name="ones")
+        bias_rows = keep.tile([P, 2 * FEATURES], BF16, name="bias_rows")
+        bias_all = keep.tile([P, 2 * FEATURES], F32, name="bias_all")
+        bias_cols = {"q": slice(0, FEATURES), "k": slice(FEATURES, 2 * FEATURES)}
+        position_int = keep.tile([P, 1], I32, name="position_int")
+        position = keep.tile([P, 1], F32, name="position")
+        freq = keep.tile([P, PAIRS], F32, name="freq")
+        angle = keep.tile([P, PAIRS], F32, name="angle")
+        turns = keep.tile([P, PAIRS], F32, name="turns")
+        part = keep.tile([P, PAIRS], F32, name="part")
+        reduced = keep.tile([P, PAIRS], F32, name="reduced")
+        cos_arg = keep.tile([P, PAIRS], F32, name="cos_arg")
+        cos_own = keep.tile([P, FEATURES], F32, name="cos_own")
+        sin_other = keep.tile([P, FEATURES], F32, name="sin_other")
+
+        x_raw = {}
+        x_sorted = {}
+
+        def load_x(r):
+            for m in range(SEQUENCES):
+                x_raw[(r, m)] = raw_pool.tile([P, ROUND_K], BF16, name="x_raw_%d" % m)
+                nc.sync.dma_start(out=x_raw[(r, m)][:], in_=x[m, :, r * ROUND_K : (r + 1) * ROUND_K])
+
+        def zero_planes(run):
+            nc.vector.memset(w_planes[run][:].rearrange("p g n -> p (g n)").bitcast(I32), 0)
+
+        def load_scale_rows(w, run):
+            groups = slice(run * SCALE_ROUNDS * ROUND, (run + 1) * SCALE_ROUNDS * ROUND)
+            rows = dram_scales[w][groups].rearrange("g (Q i) n -> i Q g n", i=4)
+            for i in range(4):
+                nc.sync.dma_start(out=w_planes[run][:].bitcast(I32)[i:P:32, :, :], in_=rows[i])
+
+        def load_words(w, r):
+            nc.sync.dma_start(
+                out=w_words[(w, r)][:].bitcast(I32),
+                in_=dram_words[w][r * ROUND : (r + 1) * ROUND].rearrange("g p n -> p g n"),
+            )
+
+        def load_weight(w, r):
+            if r % SCALE_ROUNDS == 0:
+                load_scale_rows(w, r // SCALE_ROUNDS)
+            load_words(w, r)
+
+        def sort_words(r):
+            x_sorted[r] = sorted_pool.tile([P, SEQUENCES, ROUND, 2, P], F32, name="x_sorted")
+            for m in range(SEQUENCES):
+                nc.scalar.copy(
+                    out=x_sorted[r][:, m],
+                    in_=x_raw[(r, m)][:].bitcast(F32).rearrange("p (g w u) -> p g u w", g=ROUND, u=2),
+                )
+
+        def transpose_and_quantise(r):
+            grouped = grouped_pool.tile(
+                [P, ROUND * SEQUENCES * P * PACK], BF16, name="grouped", align_bytes=64
+            )
+            grouped_pairs = grouped[:].bitcast(F32).rearrange(
+                "p (g m t u) -> p g m t u", g=ROUND, m=SEQUENCES, u=2
+            )
+            for g in range(ROUND):
+                bank = bank_pool.tile([P, SEQUENCES, 2, P], F32, name="bank")
+                for m in range(SEQUENCES):
+                    for u in range(2):
+                        nc.tensor.transpose(bank[:, m, u, :], x_sorted[r][:, m, g, u, :], identity[:])
+                nc.vector.tensor_copy(
+                    out=grouped_pairs[:, g], in_=bank[:].rearrange("p m u t -> p m t u")
+                )
+            nc.vector.quantize_mx(
+                out=x_words[r][:].rearrange("p g m t -> p (g m t)").bitcast(FP8X4),
+                scales=x_planes[r][:].rearrange("p g m t -> p (g m t)"),
+                in_=grouped[:],
+            )
+
+        def project(w, m, group):
+            r, g = divmod(group, ROUND)
+            run, plane = divmod(group, SCALE_ROUNDS * ROUND)
+            nc.tensor.matmul_mx(
+                out=acc[(w, m)][:],
+                lhsT=x_words[r][:, g, m, :].bitcast(FP8X4),
+                lhsT_scale=x_planes[r][:, g, m, :],
+                rhs=w_words[(w, r)][:, g, :].bitcast(FP4X4),
+                rhs_scale=w_planes[run][:, plane, :],
+                start=(group == 0),
+                stop=(group == GROUPS - 1),
+            )
+
+        def rotate_and_store(w, m):
+            v = rope_pool.tile([P, FEATURES], F32, name="v")
+            own = rope_pool.tile([P, FEATURES], F32, name="own")
+            other = rope_pool.tile([P, FEATURES], F32, name="other")
+            result = rope_pool.tile([P, FEATURES], F32, name="result")
+            nc.vector.tensor_add(out=v[:], in0=acc[(w, m)][:], in1=bias_all[:, bias_cols[w]])
+            nc.vector.tensor_mul(out=own[:], in0=v[:], in1=cos_own[:])
+            nc.vector.tensor_mul(out=other[:], in0=v[:], in1=sin_other[:])
+            nc.vector.tensor_add(out=result[:, :HALF], in0=own[:, :HALF], in1=other[:, HALF:])
+            nc.vector.tensor_add(out=result[:, HALF:], in0=own[:, HALF:], in1=other[:, :HALF])
+            nc.sync.dma_start(out=dram_out[w][m], in_=result[:])
+
+        nc.gpsimd.iota(position_int[:], pattern=[[0, 1]], base=0, channel_multiplier=1)
+        make_identity(nc, identity[:])
+
+        zero_planes(0)
+        nc.vector.memset(bias_rows[:].bitcast(I32), 0)
+        for w in ("q", "k"):
+            nc.scalar.dma_start(out=bias_rows[0:1, bias_cols[w]], in_=dram_bias[w].unsqueeze(0))
+
+        load_x(0)
+        load_x(1)
+        load_weight("q", 0)
+
+        nc.vector.memset(ones[:], 1.0)
+        nc.vector.memset(freq[:, 0:1], 1.0)
+        nc.vector.tensor_copy(out=position[:], in_=position_int[:])
+        for doubling in range(PAIR_BITS):
+            n = 2**doubling
+            nc.vector.tensor_scalar_mul(
+                out=freq[:, n : 2 * n], in0=freq[:, 0:n], scalar1=ROPE_BASE ** (-n / PAIRS)
+            )
+        nc.vector.tensor_scalar_mul(out=angle[:], in0=freq[:], scalar1=position[:, 0:1])
+        nc.vector.tensor_scalar(
+            out=turns[:], in0=angle[:], scalar1=1.0 / TWO_PI, scalar2=ROUND_TO_INTEGER,
+            op0=ALU.mult, op1=ALU.add,
+        )
+        nc.vector.tensor_scalar_sub(out=turns[:], in0=turns[:], scalar1=ROUND_TO_INTEGER)
+        nc.vector.scalar_tensor_tensor(
+            out=part[:], in0=turns[:], scalar=-TWO_PI_HIGH, in1=angle[:], op0=ALU.mult, op1=ALU.add
+        )
+        nc.vector.scalar_tensor_tensor(
+            out=reduced[:], in0=turns[:], scalar=-TWO_PI_LOW, in1=part[:], op0=ALU.mult, op1=ALU.add
+        )
+        nc.vector.scalar_tensor_tensor(
+            out=cos_arg[:], in0=reduced[:], scalar=-1.0, in1=reduced[:], op0=ALU.mult, op1=ALU.min
+        )
+        nc.vector.tensor_scalar_add(out=cos_arg[:], in0=cos_arg[:], scalar1=0.5 * math.pi)
+        for run in range(1, ROUNDS // SCALE_ROUNDS):
+            zero_planes(run)
+
+        for m, w in enumerate(("q", "k")):
+            nc.tensor.matmul(
+                out=acc[("k", m)][:], lhsT=ones[:], rhs=bias_rows[:, bias_cols[w]], start=True, stop=True
+            )
+            nc.vector.tensor_copy(out=bias_all[:, bias_cols[w]], in_=acc[("k", m)][:])
+
+        sort_words(0)
+        sort_words(1)
+
+        def twice(columns):
+            return columns.unsqueeze(2).to_broadcast([P, columns.shape[1], 2])
+
+        def by_pair(columns):
+            return columns.rearrange("p (j e) -> p j e", e=2)
+
+        nc.scalar.activation(out=by_pair(cos_own[:]), in_=twice(cos_arg[:]), func=ACT.Sin, scale=1.0)
+        nc.scalar.activation(
+            out=by_pair(sin_other[:, :HALF]), in_=twice(reduced[:, PAIRS // 2 :]), func=ACT.Sin, scale=1.0
+        )
+        nc.scalar.activation(
+            out=by_pair(sin_other[:, HALF:]), in_=twice(reduced[:, : PAIRS // 2]), func=ACT.Sin, scale=-1.0
+        )
+
+        transpose_and_quantise(0)
+        for r in range(ROUNDS):
+            if r + 2 < ROUNDS:
+                load_x(r + 2)
+            if r + 1 < ROUNDS:
+                load_weight("q", r + 1)
+            if r + 2 < ROUNDS:
+                sort_words(r + 2)
+            if r + 1 < ROUNDS:
+                transpose_and_quantise(r + 1)
+            for g in range(r * ROUND, (r + 1) * ROUND):
+                for m in range(SEQUENCES):
+                    project("q", m, g)
+
+        for r in range(ROUNDS):
+            load_weight("k", r)
+        for m in range(SEQUENCES):
+            rotate_and_store("q", m)
+        for g in range((ROUNDS - LAST_ROUNDS) * ROUND):
+            for m in range(SEQUENCES):
+                project("k", m, g)
+        for m in range(SEQUENCES):
+            for g in range((ROUNDS - LAST_ROUNDS) * ROUND, GROUPS):
+                project("k", m, g)
+            rotate_and_store("k", m)

@@ -31,6 +31,7 @@ ROUND = 4
 ROUNDS = GROUPS // ROUND
 ROUND_K = ROUND * K_GROUP
 SCALE_ROUNDS = 2
+K_LAG = 4
 LAST_ROUNDS = 2
 
 TWO_PI = 2.0 * math.pi
@@ -166,7 +167,7 @@ def tile_ropemultiheadattention_pa_k_kernel(
                 stop=(group == GROUPS - 1),
             )
 
-        def rotate_and_store(w, m):
+        def rotate_and_store(w, m, queue):
             v = rope_pool.tile([P, FEATURES], F32, name="v")
             own = rope_pool.tile([P, FEATURES], F32, name="own")
             other = rope_pool.tile([P, FEATURES], F32, name="other")
@@ -176,7 +177,7 @@ def tile_ropemultiheadattention_pa_k_kernel(
             nc.vector.tensor_mul(out=other[:], in0=v[:], in1=sin_other[:])
             nc.vector.tensor_add(out=result[:, :HALF], in0=own[:, :HALF], in1=other[:, HALF:])
             nc.vector.tensor_add(out=result[:, HALF:], in0=own[:, HALF:], in1=other[:, :HALF])
-            nc.sync.dma_start(out=dram_out[w][m], in_=result[:])
+            queue.dma_start(out=dram_out[w][m], in_=result[:])
 
         nc.gpsimd.iota(position_int[:], pattern=[[0, 1]], base=0, channel_multiplier=1)
         make_identity(nc, identity[:])
@@ -241,27 +242,30 @@ def tile_ropemultiheadattention_pa_k_kernel(
         )
 
         transpose_and_quantise(0)
-        for r in range(ROUNDS):
-            if r + 2 < ROUNDS:
-                load_x(r + 2)
-            if r + 1 < ROUNDS:
-                load_weight("q", r + 1)
-            if r + 2 < ROUNDS:
-                sort_words(r + 2)
-            if r + 1 < ROUNDS:
-                transpose_and_quantise(r + 1)
-            for g in range(r * ROUND, (r + 1) * ROUND):
+        for step in range(ROUNDS + K_LAG):
+            k_round = step - K_LAG
+            if step + 2 < ROUNDS:
+                load_x(step + 2)
+            if step + 1 < ROUNDS:
+                load_weight("q", step + 1)
+            if 0 <= k_round + 1 < ROUNDS:
+                load_weight("k", k_round + 1)
+            if step + 2 < ROUNDS:
+                sort_words(step + 2)
+            if step + 1 < ROUNDS:
+                transpose_and_quantise(step + 1)
+            if step < ROUNDS:
+                for group in range(step * ROUND, (step + 1) * ROUND):
+                    for m in range(SEQUENCES):
+                        project("q", m, group)
+            if step == ROUNDS - 1:
                 for m in range(SEQUENCES):
-                    project("q", m, g)
-
-        for r in range(ROUNDS):
-            load_weight("k", r)
+                    rotate_and_store("q", m, nc.scalar)
+            if 0 <= k_round < ROUNDS - LAST_ROUNDS:
+                for group in range(k_round * ROUND, (k_round + 1) * ROUND):
+                    for m in range(SEQUENCES):
+                        project("k", m, group)
         for m in range(SEQUENCES):
-            rotate_and_store("q", m)
-        for g in range((ROUNDS - LAST_ROUNDS) * ROUND):
-            for m in range(SEQUENCES):
-                project("k", m, g)
-        for m in range(SEQUENCES):
-            for g in range((ROUNDS - LAST_ROUNDS) * ROUND, GROUPS):
-                project("k", m, g)
-            rotate_and_store("k", m)
+            for group in range((ROUNDS - LAST_ROUNDS) * ROUND, GROUPS):
+                project("k", m, group)
+            rotate_and_store("k", m, nc.sync)

@@ -30,9 +30,11 @@ ROPE_BASE = 10000.0
 ROUND = 4
 ROUNDS = GROUPS // ROUND
 ROUND_K = ROUND * K_GROUP
+GROUP_COLUMNS = SEQUENCES * K_GROUP
 SCALE_ROUNDS = 2
-K_LAG = 4
-LAST_ROUNDS = 2
+SCALE_RUNS = ROUNDS // SCALE_ROUNDS
+K_LAG = 3
+LAST_ROUNDS = 3
 
 TWO_PI = 2.0 * math.pi
 TWO_PI_HIGH = 6.28125
@@ -72,10 +74,11 @@ def tile_ropemultiheadattention_pa_k_kernel(
             x_words[r] = keep.tile([P, ROUND, SEQUENCES, P], U32, name="x_words_%d" % r, align_bytes=64)
             x_planes[r] = keep.tile([P, ROUND, SEQUENCES, P], U8, name="x_planes_%d" % r, align_bytes=64)
         w_planes = {}
-        for run in range(ROUNDS // SCALE_ROUNDS):
-            w_planes[run] = keep.tile(
-                [P, SCALE_ROUNDS * ROUND, FEATURES], U8, name="w_planes_%d" % run, align_bytes=64
-            )
+        for run in range(SCALE_RUNS):
+            for w in ("q", "k"):
+                w_planes[(w, run)] = keep.tile(
+                    [P, SCALE_ROUNDS * ROUND, FEATURES], U8, name="w_planes_%s%d" % (w, run), align_bytes=64
+                )
         acc = {}
         for w in ("q", "k"):
             for m in range(SEQUENCES):
@@ -105,14 +108,14 @@ def tile_ropemultiheadattention_pa_k_kernel(
                 x_raw[(r, m)] = raw_pool.tile([P, ROUND_K], BF16, name="x_raw_%d" % m)
                 nc.sync.dma_start(out=x_raw[(r, m)][:], in_=x[m, :, r * ROUND_K : (r + 1) * ROUND_K])
 
-        def zero_planes(run):
-            nc.vector.memset(w_planes[run][:].rearrange("p g n -> p (g n)").bitcast(I32), 0)
+        def zero_planes(w, run):
+            nc.vector.memset(w_planes[(w, run)][:].rearrange("p g n -> p (g n)").bitcast(I32), 0)
 
         def load_scale_rows(w, run):
             groups = slice(run * SCALE_ROUNDS * ROUND, (run + 1) * SCALE_ROUNDS * ROUND)
             rows = dram_scales[w][groups].rearrange("g (Q i) n -> i Q g n", i=4)
             for i in range(4):
-                nc.sync.dma_start(out=w_planes[run][:].bitcast(I32)[i:P:32, :, :], in_=rows[i])
+                nc.sync.dma_start(out=w_planes[(w, run)][:].bitcast(I32)[i:P:32, :, :], in_=rows[i])
 
         def load_words(w, r):
             nc.sync.dma_start(
@@ -145,14 +148,19 @@ def tile_ropemultiheadattention_pa_k_kernel(
                 for m in range(SEQUENCES):
                     for u in range(2):
                         nc.tensor.transpose(bank[:, m, u, :], x_sorted[r][:, m, g, u, :], identity[:])
-                nc.vector.tensor_copy(
-                    out=grouped_pairs[:, g], in_=bank[:].rearrange("p m u t -> p m t u")
-                )
-            nc.vector.quantize_mx(
-                out=x_words[r][:].rearrange("p g m t -> p (g m t)").bitcast(FP8X4),
-                scales=x_planes[r][:].rearrange("p g m t -> p (g m t)"),
-                in_=grouped[:],
-            )
+                if g < ROUND - 1:
+                    nc.vector.tensor_copy(
+                        out=grouped_pairs[:, g], in_=bank[:].rearrange("p m u t -> p m t u")
+                    )
+                else:
+                    nc.scalar.copy(out=grouped_pairs[:, g], in_=bank[:].rearrange("p m u t -> p m t u"))
+                if g % 2 == 1:
+                    done = slice(g - 1, g + 1)
+                    nc.vector.quantize_mx(
+                        out=x_words[r][:, done].rearrange("p g m t -> p (g m t)").bitcast(FP8X4),
+                        scales=x_planes[r][:, done].rearrange("p g m t -> p (g m t)"),
+                        in_=grouped[:, (g - 1) * GROUP_COLUMNS : (g + 1) * GROUP_COLUMNS],
+                    )
 
         def project(w, m, group):
             r, g = divmod(group, ROUND)
@@ -162,27 +170,32 @@ def tile_ropemultiheadattention_pa_k_kernel(
                 lhsT=x_words[r][:, g, m, :].bitcast(FP8X4),
                 lhsT_scale=x_planes[r][:, g, m, :],
                 rhs=w_words[(w, r)][:, g, :].bitcast(FP4X4),
-                rhs_scale=w_planes[run][:, plane, :],
+                rhs_scale=w_planes[(w, run)][:, plane, :],
                 start=(group == 0),
                 stop=(group == GROUPS - 1),
             )
 
-        def rotate_and_store(w, m, queue):
+        results = {}
+
+        def rotate(w, m):
             v = rope_pool.tile([P, FEATURES], F32, name="v")
             own = rope_pool.tile([P, FEATURES], F32, name="own")
             other = rope_pool.tile([P, FEATURES], F32, name="other")
-            result = rope_pool.tile([P, FEATURES], F32, name="result")
+            result = keep.tile([P, FEATURES], F32, name="result_%s%d" % (w, m))
+            results[(w, m)] = result
             nc.vector.tensor_add(out=v[:], in0=acc[(w, m)][:], in1=bias_all[:, bias_cols[w]])
             nc.vector.tensor_mul(out=own[:], in0=v[:], in1=cos_own[:])
             nc.vector.tensor_mul(out=other[:], in0=v[:], in1=sin_other[:])
             nc.vector.tensor_add(out=result[:, :HALF], in0=own[:, :HALF], in1=other[:, HALF:])
             nc.vector.tensor_add(out=result[:, HALF:], in0=own[:, HALF:], in1=other[:, :HALF])
-            queue.dma_start(out=dram_out[w][m], in_=result[:])
+
+        def store(w, m):
+            nc.sync.dma_start(out=dram_out[w][m], in_=results[(w, m)][:])
 
         nc.gpsimd.iota(position_int[:], pattern=[[0, 1]], base=0, channel_multiplier=1)
         make_identity(nc, identity[:])
 
-        zero_planes(0)
+        zero_planes("q", 0)
         nc.vector.memset(bias_rows[:].bitcast(I32), 0)
         for w in ("q", "k"):
             nc.scalar.dma_start(out=bias_rows[0:1, bias_cols[w]], in_=dram_bias[w].unsqueeze(0))
@@ -215,8 +228,8 @@ def tile_ropemultiheadattention_pa_k_kernel(
             out=cos_arg[:], in0=reduced[:], scalar=-1.0, in1=reduced[:], op0=ALU.mult, op1=ALU.min
         )
         nc.vector.tensor_scalar_add(out=cos_arg[:], in0=cos_arg[:], scalar1=0.5 * math.pi)
-        for run in range(1, ROUNDS // SCALE_ROUNDS):
-            zero_planes(run)
+        for run in range(1, SCALE_RUNS):
+            zero_planes("q", run)
 
         for m, w in enumerate(("q", "k")):
             nc.tensor.matmul(
@@ -254,18 +267,23 @@ def tile_ropemultiheadattention_pa_k_kernel(
                 sort_words(step + 2)
             if step + 1 < ROUNDS:
                 transpose_and_quantise(step + 1)
+            if step < SCALE_RUNS:
+                zero_planes("k", step)
             if step < ROUNDS:
                 for group in range(step * ROUND, (step + 1) * ROUND):
                     for m in range(SEQUENCES):
                         project("q", m, group)
             if step == ROUNDS - 1:
                 for m in range(SEQUENCES):
-                    rotate_and_store("q", m, nc.scalar)
+                    rotate("q", m)
             if 0 <= k_round < ROUNDS - LAST_ROUNDS:
                 for group in range(k_round * ROUND, (k_round + 1) * ROUND):
                     for m in range(SEQUENCES):
                         project("k", m, group)
         for m in range(SEQUENCES):
+            store("q", m)
+        for m in range(SEQUENCES):
             for group in range((ROUNDS - LAST_ROUNDS) * ROUND, GROUPS):
                 project("k", m, group)
-            rotate_and_store("k", m, nc.sync)
+            rotate("k", m)
+            store("k", m)

@@ -34,6 +34,9 @@ GROUP_COLUMNS = SEQUENCES * K_GROUP
 SCALE_ROUNDS = 2
 SCALE_RUNS = ROUNDS // SCALE_ROUNDS
 K_LAG = 3
+LATER_ZEROS = (("k", 0), ("q", 2), ("k", 1), ("q", 3), ("k", 2), ("k", 3))
+TABLE_STEP = 3
+BIAS_STEP = 1
 LAST_ROUNDS = 3
 
 TWO_PI = 2.0 * math.pi
@@ -228,14 +231,14 @@ def tile_ropemultiheadattention_pa_k_kernel(
             out=cos_arg[:], in0=reduced[:], scalar=-1.0, in1=reduced[:], op0=ALU.mult, op1=ALU.min
         )
         nc.vector.tensor_scalar_add(out=cos_arg[:], in0=cos_arg[:], scalar1=0.5 * math.pi)
-        for run in range(1, SCALE_RUNS):
-            zero_planes("q", run)
+        zero_planes("q", 1)
 
-        for m, w in enumerate(("q", "k")):
-            nc.tensor.matmul(
-                out=acc[("k", m)][:], lhsT=ones[:], rhs=bias_rows[:, bias_cols[w]], start=True, stop=True
-            )
-            nc.vector.tensor_copy(out=bias_all[:, bias_cols[w]], in_=acc[("k", m)][:])
+        def spread_biases():
+            for m, w in enumerate(("q", "k")):
+                nc.tensor.matmul(
+                    out=acc[("k", m)][:], lhsT=ones[:], rhs=bias_rows[:, bias_cols[w]], start=True, stop=True
+                )
+                nc.vector.tensor_copy(out=bias_all[:, bias_cols[w]], in_=acc[("k", m)][:])
 
         sort_words(0)
         sort_words(1)
@@ -246,13 +249,14 @@ def tile_ropemultiheadattention_pa_k_kernel(
         def by_pair(columns):
             return columns.rearrange("p (j e) -> p j e", e=2)
 
-        nc.scalar.activation(out=by_pair(cos_own[:]), in_=twice(cos_arg[:]), func=ACT.Sin, scale=1.0)
-        nc.scalar.activation(
-            out=by_pair(sin_other[:, :HALF]), in_=twice(reduced[:, PAIRS // 2 :]), func=ACT.Sin, scale=1.0
-        )
-        nc.scalar.activation(
-            out=by_pair(sin_other[:, HALF:]), in_=twice(reduced[:, : PAIRS // 2]), func=ACT.Sin, scale=-1.0
-        )
+        def cos_and_sin():
+            nc.scalar.activation(out=by_pair(cos_own[:]), in_=twice(cos_arg[:]), func=ACT.Sin, scale=1.0)
+            nc.scalar.activation(
+                out=by_pair(sin_other[:, :HALF]), in_=twice(reduced[:, PAIRS // 2 :]), func=ACT.Sin, scale=1.0
+            )
+            nc.scalar.activation(
+                out=by_pair(sin_other[:, HALF:]), in_=twice(reduced[:, : PAIRS // 2]), func=ACT.Sin, scale=-1.0
+            )
 
         transpose_and_quantise(0)
         for step in range(ROUNDS + K_LAG):
@@ -267,12 +271,16 @@ def tile_ropemultiheadattention_pa_k_kernel(
                 sort_words(step + 2)
             if step + 1 < ROUNDS:
                 transpose_and_quantise(step + 1)
-            if step < SCALE_RUNS:
-                zero_planes("k", step)
+            if step < len(LATER_ZEROS):
+                zero_planes(*LATER_ZEROS[step])
+            if step == TABLE_STEP:
+                cos_and_sin()
             if step < ROUNDS:
                 for group in range(step * ROUND, (step + 1) * ROUND):
                     for m in range(SEQUENCES):
                         project("q", m, group)
+            if step == BIAS_STEP:
+                spread_biases()
             if step == ROUNDS - 1:
                 for m in range(SEQUENCES):
                     rotate("q", m)

@@ -114,11 +114,12 @@ def tile_ropemultiheadattention_pa_k_kernel(
         def zero_planes(w, run):
             nc.vector.memset(w_planes[(w, run)][:].rearrange("p g n -> p (g n)").bitcast(I32), 0)
 
-        def load_scale_rows(w, run):
-            groups = slice(run * SCALE_ROUNDS * ROUND, (run + 1) * SCALE_ROUNDS * ROUND)
-            rows = dram_scales[w][groups].rearrange("g (Q i) n -> i Q g n", i=4)
+        def load_scale_rows(w, r):
+            rows = dram_scales[w][r * ROUND : (r + 1) * ROUND].rearrange("g (Q i) n -> i Q g n", i=4)
+            run, part = divmod(r, SCALE_ROUNDS)
+            planes = slice(part * ROUND, (part + 1) * ROUND)
             for i in range(4):
-                nc.sync.dma_start(out=w_planes[(w, run)][:].bitcast(I32)[i:P:32, :, :], in_=rows[i])
+                nc.sync.dma_start(out=w_planes[(w, run)][:].bitcast(I32)[i:P:32, planes, :], in_=rows[i])
 
         def load_words(w, r):
             nc.sync.dma_start(
@@ -127,8 +128,7 @@ def tile_ropemultiheadattention_pa_k_kernel(
             )
 
         def load_weight(w, r):
-            if r % SCALE_ROUNDS == 0:
-                load_scale_rows(w, r // SCALE_ROUNDS)
+            load_scale_rows(w, r)
             load_words(w, r)
 
         def sort_words(r):

@@ -115,11 +115,13 @@ def tile_ropemultiheadattention_pa_k_kernel(
             nc.vector.memset(w_planes[(w, run)][:].rearrange("p g n -> p (g n)").bitcast(I32), 0)
 
         def load_scale_rows(w, r):
-            rows = dram_scales[w][r * ROUND : (r + 1) * ROUND].rearrange("g (Q i) n -> i Q g n", i=4)
+            rows = dram_scales[w][r * ROUND : (r + 1) * ROUND].rearrange("g (Q i) n -> Q i g n", i=4)
             run, part = divmod(r, SCALE_ROUNDS)
             planes = slice(part * ROUND, (part + 1) * ROUND)
-            for i in range(4):
-                nc.sync.dma_start(out=w_planes[(w, run)][:].bitcast(I32)[i:P:32, planes, :], in_=rows[i])
+            for Q in (0, 2, 1, 3):
+                nc.sync.dma_start(
+                    out=w_planes[(w, run)][:].bitcast(I32)[32 * Q : 32 * Q + 4, planes, :], in_=rows[Q]
+                )
 
         def load_words(w, r):
             nc.sync.dma_start(

import math
from contextlib import ExitStack

import concourse.mybir as mybir
from concourse.masks import make_identity

F32 = mybir.dt.float32
BF16 = mybir.dt.bfloat16
I32 = mybir.dt.int32
U32 = mybir.dt.uint32
U8 = mybir.dt.uint8
FP8X4 = mybir.dt.float8_e4m3fn_x4
FP4X4 = mybir.dt.float4_e2m1fn_x4
ALU = mybir.AluOpType
ACT = mybir.ActivationFunctionType

P = 128
PACK = 4
K_GROUP = P * PACK
SEQUENCES = 2
K = 16384
GROUPS = K // K_GROUP
FEATURES = 512
HALF = FEATURES // 2
PAIRS = FEATURES // 2
PAIR_BITS = 8
assert 2**PAIR_BITS == PAIRS
ROPE_BASE = 10000.0

ROUND = 4
ROUNDS = GROUPS // ROUND
ROUND_K = ROUND * K_GROUP
GROUP_COLUMNS = SEQUENCES * K_GROUP
SCALE_ROUNDS = 2
SCALE_RUNS = ROUNDS // SCALE_ROUNDS
K_LAG = 3
LATER_ZEROS = (("k", 0), ("q", 2), ("k", 1), ("q", 3), ("k", 2), ("k", 3))
TABLE_STEP = 3
BIAS_STEP = 1
LAST_ROUNDS = 3

TWO_PI = 2.0 * math.pi
TWO_PI_HIGH = 6.28125
TWO_PI_LOW = TWO_PI - TWO_PI_HIGH
ROUND_TO_INTEGER = 12582912.0

FLOPS = 2 * SEQUENCES * P * K * 2 * FEATURES


def tile_ropemultiheadattention_pa_k_kernel(
    tc, x, Wq_words, Wq_scales, bq, Wk_words, Wk_scales, bk, out_0, out_1
):
    nc = tc.nc
    dram_words = {"q": Wq_words.bitcast(I32), "k": Wk_words.bitcast(I32)}
    dram_scales = {"q": Wq_scales.bitcast(I32), "k": Wk_scales.bitcast(I32)}
    dram_bias = {"q": bq, "k": bk}
    dram_out = {"q": out_0, "k": out_1}

    with ExitStack() as ctx:
        keep = ctx.enter_context(tc.tile_pool(name="keep", bufs=1))
        raw_pool = ctx.enter_context(tc.tile_pool(name="raw", bufs=3))
        sorted_pool = ctx.enter_context(tc.tile_pool(name="sorted", bufs=2))
        grouped_pool = ctx.enter_context(tc.tile_pool(name="grouped", bufs=2))
        rope_pool = ctx.enter_context(tc.tile_pool(name="rope", bufs=2))
        acc_pool = ctx.enter_context(tc.psum_pool(name="acc", bufs=1))
        bank_pool = ctx.enter_context(tc.psum_pool(name="bank", bufs=4))
        ctx.enter_context(tc.manual_schedule())

        w_words = {}
        x_words = {}
        x_planes = {}
        for r in range(ROUNDS):
            for w in ("q", "k"):
                w_words[(w, r)] = keep.tile(
                    [P, ROUND, 2 * FEATURES], U8, name="w_words_%s%d" % (w, r), align_bytes=64
                )
            x_words[r] = keep.tile([P, ROUND, SEQUENCES, P], U32, name="x_words_%d" % r, align_bytes=64)
            x_planes[r] = keep.tile([P, ROUND, SEQUENCES, P], U8, name="x_planes_%d" % r, align_bytes=64)
        w_planes = {}
        for run in range(SCALE_RUNS):
            for w in ("q", "k"):
                w_planes[(w, run)] = keep.tile(
                    [P, SCALE_ROUNDS * ROUND, FEATURES], U8, name="w_planes_%s%d" % (w, run), align_bytes=64
                )
        acc = {}
        for w in ("q", "k"):
            for m in range(SEQUENCES):
                acc[(w, m)] = acc_pool.tile([P, FEATURES], F32, name="acc_%s%d" % (w, m))

        identity = keep.tile([P, P], F32, name="identity")
        ones = keep.tile([P, P], BF16, name="ones")
        bias_rows = keep.tile([P, 2 * FEATURES], BF16, name="bias_rows")
        bias_all = keep.tile([P, 2 * FEATURES], F32, name="bias_all")
        bias_cols = {"q": slice(0, FEATURES), "k": slice(FEATURES, 2 * FEATURES)}
        position_int = keep.tile([P, 1], I32, name="position_int")
        position = keep.tile([P, 1], F32, name="position")
        freq = keep.tile([P, PAIRS], F32, name="freq")
        angle = keep.tile([P, PAIRS], F32, name="angle")
        turns = keep.tile([P, PAIRS], F32, name="turns")
        part = keep.tile([P, PAIRS], F32, name="part")
        reduced = keep.tile([P, PAIRS], F32, name="reduced")
        cos_arg = keep.tile([P, PAIRS], F32, name="cos_arg")
        cos_own = keep.tile([P, FEATURES], F32, name="cos_own")
        sin_other = keep.tile([P, FEATURES], F32, name="sin_other")

        x_raw = {}
        x_sorted = {}

        def load_x(r):
            for m in range(SEQUENCES):
                x_raw[(r, m)] = raw_pool.tile([P, ROUND_K], BF16, name="x_raw_%d" % m)
                nc.sync.dma_start(out=x_raw[(r, m)][:], in_=x[m, :, r * ROUND_K : (r + 1) * ROUND_K])

        def zero_planes(w, run):
            nc.vector.memset(w_planes[(w, run)][:].rearrange("p g n -> p (g n)").bitcast(I32), 0)

        def load_scale_rows(w, r):
            rows = dram_scales[w][r * ROUND : (r + 1) * ROUND].rearrange("g (Q i) n -> Q i g n", i=4)
            run, part = divmod(r, SCALE_ROUNDS)
            planes = slice(part * ROUND, (part + 1) * ROUND)
            for Q in (0, 2, 1, 3):
                nc.sync.dma_start(
                    out=w_planes[(w, run)][:].bitcast(I32)[32 * Q : 32 * Q + 4, planes, :], in_=rows[Q]
                )

        def load_words(w, r):
            nc.sync.dma_start(
                out=w_words[(w, r)][:].bitcast(I32),
                in_=dram_words[w][r * ROUND : (r + 1) * ROUND].rearrange("g p n -> p g n"),
            )

        def load_weight(w, r):
            load_scale_rows(w, r)
            load_words(w, r)

        def sort_words(r):
            x_sorted[r] = sorted_pool.tile([P, SEQUENCES, ROUND, 2, P], F32, name="x_sorted")
            for m in range(SEQUENCES):
                nc.scalar.copy(
                    out=x_sorted[r][:, m],
                    in_=x_raw[(r, m)][:].bitcast(F32).rearrange("p (g w u) -> p g u w", g=ROUND, u=2),
                )

        def transpose_and_quantise(r):
            grouped = grouped_pool.tile(
                [P, ROUND * SEQUENCES * P * PACK], BF16, name="grouped", align_bytes=64
            )
            grouped_pairs = grouped[:].bitcast(F32).rearrange(
                "p (g m t u) -> p g m t u", g=ROUND, m=SEQUENCES, u=2
            )
            for g in range(ROUND):
                bank = bank_pool.tile([P, SEQUENCES, 2, P], F32, name="bank")
                for m in range(SEQUENCES):
                    for u in range(2):
                        nc.tensor.transpose(bank[:, m, u, :], x_sorted[r][:, m, g, u, :], identity[:])
                if g < ROUND - 1:
                    nc.vector.tensor_copy(
                        out=grouped_pairs[:, g], in_=bank[:].rearrange("p m u t -> p m t u")
                    )
                else:
                    nc.scalar.copy(out=grouped_pairs[:, g], in_=bank[:].rearrange("p m u t -> p m t u"))
                if g % 2 == 1:
                    done = slice(g - 1, g + 1)
                    nc.vector.quantize_mx(
                        out=x_words[r][:, done].rearrange("p g m t -> p (g m t)").bitcast(FP8X4),
                        scales=x_planes[r][:, done].rearrange("p g m t -> p (g m t)"),
                        in_=grouped[:, (g - 1) * GROUP_COLUMNS : (g + 1) * GROUP_COLUMNS],
                    )

        def project(w, m, group):
            r, g = divmod(group, ROUND)
            run, plane = divmod(group, SCALE_ROUNDS * ROUND)
            nc.tensor.matmul_mx(
                out=acc[(w, m)][:],
                lhsT=x_words[r][:, g, m, :].bitcast(FP8X4),
                lhsT_scale=x_planes[r][:, g, m, :],
                rhs=w_words[(w, r)][:, g, :].bitcast(FP4X4),
                rhs_scale=w_planes[(w, run)][:, plane, :],
                start=(group == 0),
                stop=(group == GROUPS - 1),
            )

        results = {}

        def rotate(w, m):
            v = rope_pool.tile([P, FEATURES], F32, name="v")
            own = rope_pool.tile([P, FEATURES], F32, name="own")
            other = rope_pool.tile([P, FEATURES], F32, name="other")
            result = keep.tile([P, FEATURES], F32, name="result_%s%d" % (w, m))
            results[(w, m)] = result
            nc.vector.tensor_add(out=v[:], in0=acc[(w, m)][:], in1=bias_all[:, bias_cols[w]])
            nc.vector.tensor_mul(out=own[:], in0=v[:], in1=cos_own[:])
            nc.vector.tensor_mul(out=other[:], in0=v[:], in1=sin_other[:])
            nc.vector.tensor_add(out=result[:, :HALF], in0=own[:, :HALF], in1=other[:, HALF:])
            nc.vector.tensor_add(out=result[:, HALF:], in0=own[:, HALF:], in1=other[:, :HALF])

        def store(w, m):
            nc.sync.dma_start(out=dram_out[w][m], in_=results[(w, m)][:])

        nc.gpsimd.iota(position_int[:], pattern=[[0, 1]], base=0, channel_multiplier=1)
        make_identity(nc, identity[:])

        zero_planes("q", 0)
        nc.vector.memset(bias_rows[:].bitcast(I32), 0)
        for w in ("q", "k"):
            nc.scalar.dma_start(out=bias_rows[0:1, bias_cols[w]], in_=dram_bias[w].unsqueeze(0))

        load_x(0)
        load_x(1)
        load_weight("q", 0)

        nc.vector.memset(ones[:], 1.0)
        nc.vector.memset(freq[:, 0:1], 1.0)
        nc.vector.tensor_copy(out=position[:], in_=position_int[:])
        for doubling in range(PAIR_BITS):
            n = 2**doubling
            nc.vector.tensor_scalar_mul(
                out=freq[:, n : 2 * n], in0=freq[:, 0:n], scalar1=ROPE_BASE ** (-n / PAIRS)
            )
        nc.vector.tensor_scalar_mul(out=angle[:], in0=freq[:], scalar1=position[:, 0:1])
        nc.vector.tensor_scalar(
            out=turns[:], in0=angle[:], scalar1=1.0 / TWO_PI, scalar2=ROUND_TO_INTEGER,
            op0=ALU.mult, op1=ALU.add,
        )
        nc.vector.tensor_scalar_sub(out=turns[:], in0=turns[:], scalar1=ROUND_TO_INTEGER)
        nc.vector.scalar_tensor_tensor(
            out=part[:], in0=turns[:], scalar=-TWO_PI_HIGH, in1=angle[:], op0=ALU.mult, op1=ALU.add
        )
        nc.vector.scalar_tensor_tensor(
            out=reduced[:], in0=turns[:], scalar=-TWO_PI_LOW, in1=part[:], op0=ALU.mult, op1=ALU.add
        )
        nc.vector.scalar_tensor_tensor(
            out=cos_arg[:], in0=reduced[:], scalar=-1.0, in1=reduced[:], op0=ALU.mult, op1=ALU.min
        )
        nc.vector.tensor_scalar_add(out=cos_arg[:], in0=cos_arg[:], scalar1=0.5 * math.pi)
        zero_planes("q", 1)

        def spread_biases():
            for m, w in enumerate(("q", "k")):
                nc.tensor.matmul(
                    out=acc[("k", m)][:], lhsT=ones[:], rhs=bias_rows[:, bias_cols[w]], start=True, stop=True
                )
                nc.vector.tensor_copy(out=bias_all[:, bias_cols[w]], in_=acc[("k", m)][:])

        sort_words(0)
        sort_words(1)

        def twice(columns):
            return columns.unsqueeze(2).to_broadcast([P, columns.shape[1], 2])

        def by_pair(columns):
            return columns.rearrange("p (j e) -> p j e", e=2)

        def cos_and_sin():
            nc.scalar.activation(out=by_pair(cos_own[:]), in_=twice(cos_arg[:]), func=ACT.Sin, scale=1.0)
            nc.scalar.activation(
                out=by_pair(sin_other[:, :HALF]), in_=twice(reduced[:, PAIRS // 2 :]), func=ACT.Sin, scale=1.0
            )
            nc.scalar.activation(
                out=by_pair(sin_other[:, HALF:]), in_=twice(reduced[:, : PAIRS // 2]), func=ACT.Sin, scale=-1.0
            )

        transpose_and_quantise(0)
        for step in range(ROUNDS + K_LAG):
            k_round = step - K_LAG
            if step + 2 < ROUNDS:
                load_x(step + 2)
            if step + 1 < ROUNDS:
                load_weight("q", step + 1)
            if 0 <= k_round + 1 < ROUNDS:
                load_weight("k", k_round + 1)
            if step + 2 < ROUNDS:
                sort_words(step + 2)
            if step + 1 < ROUNDS:
                transpose_and_quantise(step + 1)
            if step < len(LATER_ZEROS):
                zero_planes(*LATER_ZEROS[step])
            if step == TABLE_STEP:
                cos_and_sin()
            if step < ROUNDS:
                for group in range(step * ROUND, (step + 1) * ROUND):
                    for m in range(SEQUENCES):
                        project("q", m, group)
            if step == BIAS_STEP:
                spread_biases()
            if step == ROUNDS - 1:
                for m in range(SEQUENCES):
                    rotate("q", m)
            if 0 <= k_round < ROUNDS - LAST_ROUNDS:
                for group in range(k_round * ROUND, (k_round + 1) * ROUND):
                    for m in range(SEQUENCES):
                        project("k", m, group)
        for m in range(SEQUENCES):
            store("q", m)
        for m in range(SEQUENCES):
            for group in range((ROUNDS - LAST_ROUNDS) * ROUND, GROUPS):
                project("k", m, group)
            rotate("k", m)
            store("k", m)
